import numpy as np
import ml_dtypes


def mxq(x, axis, fmt="e4m3"):
    dtype, down = {"e4m3": (ml_dtypes.float8_e4m3fn, 7), "e5m2": (ml_dtypes.float8_e5m2, 14)}[fmt]
    v = np.moveaxis(np.asarray(x, np.float32).astype(ml_dtypes.bfloat16).astype(np.float64), axis, -1)
    blocks = v.reshape(v.shape[:-1] + (-1, 32))
    amax = np.abs(blocks).max(-1, keepdims=True)
    byte = np.maximum(np.where(amax > 0, np.frexp(amax)[1] - 1 + 127, 0) - down, 1)
    scale = np.exp2(byte - 127.0)
    codes = (blocks / scale).astype(np.float32).astype(dtype).astype(np.float64)
    return np.moveaxis((codes * scale).reshape(v.shape), -1, axis)


WIDE = False


def mx_kscale(k):
    if not WIDE:
        return np.ones(k)
    levels = np.array([10, -10, 5, -5, 0])
    a = np.random.permutation(np.resize(levels, k // 512 * 4)).reshape(k // 512, 4)
    idx = np.arange(k)
    return np.exp2(a[idx // 512, idx % 128 // 32])


BF16 = ml_dtypes.bfloat16


def bf(x):
    return np.asarray(x, np.float32).astype(BF16)


def f64(x):
    return np.asarray(x).astype(np.float64)


N, CIN, COUT, V, T, S = 1, 512, 128, 32, 128, 16
EPS = 1e-5
KG = S * V


def setup_inputs():
    r = np.random.standard_normal
    c = mx_kscale(CIN)
    g = mx_kscale(KG).reshape(S, V)
    return {"ada_A": bf(r((N, CIN, V, V)) * c[None, :, None, None]),
            "ada_w": bf(r((S, COUT, CIN)) / np.sqrt(CIN) / c),
            "ada_b": bf(r((S, COUT)) * 0.3),
            "PA": bf(r((S, V, V)) * 2.0 / np.sqrt(KG) * g[:, None, :]),
            "feat": bf(r((S, N, COUT, V, T)) / g[:, None, None, :, None]),
            "bn_gamma": bf(1.0 + 0.1 * r(COUT)),
            "bn_beta": bf(0.3 * r(COUT)),
            "bn_mean": bf(0.3 * r(COUT)),
            "bn_var": bf(np.abs(r(COUT)) + 1.0),
            "res": bf(r((N, COUT, V, T)) * 0.9)}


def reference(ada_A, ada_w, ada_b, PA, feat, bn_gamma, bn_beta, bn_mean, bn_var, res):
    wq = mxq(f64(ada_w).reshape(S * COUT, CIN), 1, "e4m3")
    aq = mxq(f64(ada_A).reshape(N, CIN, V * V), 1, "e4m3")
    adaA = (wq @ aq).reshape(N, S, COUT, V, V).transpose(1, 0, 2, 3, 4) + f64(ada_b)[:, None, :, None, None]
    A_full = adaA * f64(PA)[:, None, None, :, :]
    Ag = A_full.transpose(1, 2, 3, 0, 4).reshape(N, COUT, V, KG)
    Fg = f64(feat).transpose(1, 2, 0, 3, 4).reshape(N, COUT, KG, T)
    y = mxq(Ag, 3, "e4m3") @ mxq(Fg, 2, "e4m3")
    scale = f64(bn_gamma) / np.sqrt(f64(bn_var) + EPS)
    z = (y - f64(bn_mean)[:, None, None]) * scale[:, None, None] + f64(bn_beta)[:, None, None]
    return np.maximum(z + f64(res), 0.0)

@@ -1,0 +1,361 @@
+from contextlib import ExitStack
+
+import concourse.mybir as mybir
+from concourse.masks import make_identity
+
+F32 = mybir.dt.float32
+BF16 = mybir.dt.bfloat16
+U32 = mybir.dt.uint32
+U8 = mybir.dt.uint8
+FP8X4 = mybir.dt.float8_e4m3fn_x4
+ALU = mybir.AluOpType
+ACT = mybir.ActivationFunctionType
+AX = mybir.AxisListType
+
+P = 128
+S, CIN, COUT, V, T = 16, 512, 128, 32, 128
+EPS = 1e-5
+FLOPS = 2 * S * COUT * CIN * V * V + 2 * COUT * V * S * V * T
+N_TILES = COUT // 4
+PREFETCH = 5
+
+
+def tile_multiscale_gcn_pa_kernel(
+    tc, ada_A, ada_w, ada_b, PA, feat, bn_gamma, bn_beta, bn_mean, bn_var, res, out
+):
+    nc = tc.nc
+    with ExitStack() as ctx:
+        const = ctx.enter_context(tc.tile_pool(name="const", bufs=1))
+        keep = ctx.enter_context(tc.tile_pool(name="keep", bufs=1))
+        big = ctx.enter_context(tc.tile_pool(name="big", bufs=1))
+        raw_pool = ctx.enter_context(tc.tile_pool(name="rawp", bufs=PREFETCH + 1))
+        grp_pool = ctx.enter_context(tc.tile_pool(name="grpp", bufs=4))
+        ps_m = ctx.enter_context(tc.psum_pool(name="psm", bufs=2))
+        ps_t = ctx.enter_context(tc.psum_pool(name="pst", bufs=3))
+        ps_s = ctx.enter_context(tc.psum_pool(name="pss", bufs=3))
+
+        w_codes = keep.tile([P, S * COUT], U32, align_bytes=64)
+        w_scales = keep.tile([P, S * COUT], U8, align_bytes=64)
+        a_codes = keep.tile([P, V * V], U32, align_bytes=64)
+        a_scales = keep.tile([P, V * V], U8, align_bytes=64)
+        g_codes = keep.tile([P, COUT * V], U32, align_bytes=64)
+        g_scales = keep.tile([P, COUT * V], U8, align_bytes=64)
+        f_codes = keep.tile([P, COUT * T], U32, align_bytes=64)
+        f_scales = keep.tile([P, COUT * T], U8, align_bytes=64)
+
+        ident32 = const.tile([P, P], F32)
+        make_identity(nc, ident32[:])
+        identb = const.tile([P, P], BF16)
+        make_identity(nc, identb[:])
+        zrows = const.tile([P, P], BF16)
+        nc.vector.memset(zrows[:], 0.0)
+
+        a2 = ada_A.rearrange("n i v w -> (n i) (v w)")
+
+        def load_a(h):
+            r = raw_pool.tile([P, 2048], BF16, tag="raw", name="raw_a")
+            r3 = r[:].rearrange("q (t c) -> q t c", t=4)
+            for u in range(2):
+                nc.sync.dma_start(
+                    out=r3[:, 2 * u : 2 * u + 2, :],
+                    in_=a2[256 * u : 256 * u + 256, 512 * h : 512 * h + 512].rearrange(
+                        "(q e) c -> q e c", e=2
+                    ),
+                )
+            return r
+
+        def load_w(c):
+            r = raw_pool.tile([P, 2048], BF16, tag="raw", name="raw_w")
+            nc.sync.dma_start(
+                out=r[:].rearrange("o (s i) -> o s i", s=4),
+                in_=ada_w[4 * c : 4 * c + 4].rearrange("s o i -> o s i"),
+            )
+            return r
+
+        raw_a = [load_a(0)]
+        raw_w = [load_w(0), load_w(1)]
+        nc.scalar.dma_start(out=zrows[4:20, :], in_=ada_b)
+        nc.scalar.dma_start(out=zrows[0:1, :], in_=bn_gamma.unsqueeze(0))
+        nc.scalar.dma_start(out=zrows[1:2, :], in_=bn_beta.unsqueeze(0))
+        nc.scalar.dma_start(out=zrows[2:3, :], in_=bn_mean.unsqueeze(0))
+        nc.scalar.dma_start(out=zrows[3:4, :], in_=bn_var.unsqueeze(0))
+        raw_w.append(load_w(2))
+        raw_w.append(load_w(3))
+        raw_a.append(load_a(1))
+        pa_full = const.tile([P, V * V], BF16)
+        pa_rows = PA.rearrange("s v w -> s (v w)")
+        for q in range(8):
+            nc.scalar.dma_start(out=pa_full[q:P:8, :], in_=pa_rows)
+
+        def regroup(dst, src, n, engine):
+            if engine == "v":
+                if n == 1:
+                    nc.vector.tensor_copy(
+                        out=dst.rearrange("p (c i t) -> p c t i", i=4, t=4),
+                        in_=src.rearrange("p (t c i) -> p c t i", t=4, i=4),
+                    )
+                else:
+                    nc.vector.tensor_copy(
+                        out=dst.rearrange("p (n c i t) -> p n c t i", n=n, i=4, t=4),
+                        in_=src.rearrange("p (n t c i) -> p n c t i", n=n, t=4, i=4),
+                    )
+            else:
+                w = 2048 // n
+                for b in range(n):
+                    nc.scalar.copy(
+                        out=dst[:, w * b : w * b + w].rearrange("p (c i t) -> p c t i", i=4, t=4),
+                        in_=src[:, w * b : w * b + w].rearrange("p (t c i) -> p c t i", t=4, i=4),
+                    )
+
+        zt = ps_t.tile([P, P], BF16, tag="tp", name="zt")
+        nc.tensor.transpose(zt[:], zrows[:], identb[:])
+        cst = const.tile([P, 20], F32)
+        nc.vector.tensor_copy(out=cst[:], in_=zt[:, 0:20])
+
+        def quant_a(h):
+            g = grp_pool.tile([P, 2048], BF16, tag="grp", name="grp_a", align_bytes=64)
+            regroup(g[:], raw_a[h][:], 1, "v")
+            return g
+
+        def quant_a2(h, g):
+            nc.vector.quantize_mx(
+                out=a_codes[:, 512 * h : 512 * h + 512].bitcast(FP8X4),
+                scales=a_scales[:, 512 * h : 512 * h + 512],
+                in_=g[:],
+            )
+
+        ga0 = quant_a(0)
+
+        def w_transposes(c):
+            r32 = raw_w[c][:].bitcast(F32)
+            g = grp_pool.tile([P, 2048], BF16, tag="grp", name="grp_w", align_bytes=64)
+            g32 = g[:].bitcast(F32)
+            for a in range(2):
+                wt = ps_t.tile([P, 512], F32, tag="tp", name="wt")
+                for b in range(2):
+                    for u in range(2):
+                        col = (2 * a + b) * 256 + u * 128
+                        nc.tensor.transpose(
+                            wt[:, (2 * b + u) * 128 : (2 * b + u) * 128 + 128],
+                            r32[:, col : col + 128],
+                            ident32[:],
+                        )
+                nc.scalar.copy(
+                    out=g32[:, 512 * a : 512 * a + 512].rearrange("q (b o u) -> q b o u", b=2, u=2),
+                    in_=wt[:].rearrange("q (b u o) -> q b o u", b=2, u=2),
+                )
+            return g
+
+        def w_quant(c, g):
+            nc.vector.quantize_mx(
+                out=w_codes[:, 512 * c : 512 * c + 512].bitcast(FP8X4),
+                scales=w_scales[:, 512 * c : 512 * c + 512],
+                in_=g[:],
+            )
+
+        gw0 = w_transposes(0)
+        quant_a2(0, ga0)
+        gw1 = w_transposes(1)
+        w_quant(0, gw0)
+        gw2 = w_transposes(2)
+        w_quant(1, gw1)
+        gw3 = w_transposes(3)
+        w_quant(2, gw2)
+        ga1 = quant_a(1)
+        w_quant(3, gw3)
+        quant_a2(1, ga1)
+
+        m8 = const.tile([P, 8], F32)
+        nc.vector.tensor_reduce(
+            out=m8[:], in_=ident32[:].rearrange("p (s w) -> p w s", w=8), axis=AX.X, op=ALU.add
+        )
+        pa_sel = const.tile([P, V * V], F32)
+        nc.vector.tensor_tensor(
+            out=pa_sel[:].rearrange("p (v j w) -> p v j w", v=V, j=4),
+            in0=pa_full[:].rearrange("p (v w j) -> p v j w", v=V, j=4),
+            in1=m8[:].unsqueeze(1).unsqueeze(1).to_broadcast([P, V, 4, 8]),
+            op=ALU.mult,
+        )
+        pa_t = const.tile([P, V * 4], F32)
+        nc.vector.tensor_reduce(
+            out=pa_t[:], in_=pa_sel[:].rearrange("p (c w) -> p c w", w=8), axis=AX.X, op=ALU.add
+        )
+
+        bn = const.tile([P, 8], F32)
+        nc.vector.tensor_scalar_add(out=bn[:, 0:1], in0=cst[:, 3:4], scalar1=EPS)
+        sq = const.tile([P, 1], F32)
+        nc.scalar.sqrt(out=sq[:], in_=bn[:, 0:1])
+        nc.vector.reciprocal(out=bn[:, 1:2], in_=sq[:])
+        nc.vector.tensor_tensor(out=bn[:, 2:3], in0=cst[:, 0:1], in1=bn[:, 1:2], op=ALU.mult)
+        nc.vector.tensor_tensor(out=bn[:, 3:4], in0=cst[:, 2:3], in1=bn[:, 2:3], op=ALU.mult)
+        nc.vector.tensor_tensor(out=bn[:, 4:5], in0=cst[:, 1:2], in1=bn[:, 3:4], op=ALU.subtract)
+        rep = const.tile([P, 2 * P], F32)
+        nc.vector.tensor_copy(out=rep[:, 0:P], in_=bn[:, 2:3].to_broadcast([P, P]))
+        nc.vector.tensor_copy(out=rep[:, P : 2 * P], in_=bn[:, 4:5].to_broadcast([P, P]))
+        rt = ps_t.tile([P, 2 * P], F32, tag="tp", name="rt")
+        nc.tensor.transpose(rt[:, 0:P], rep[:, 0:P], ident32[:])
+        nc.tensor.transpose(rt[:, P : 2 * P], rep[:, P : 2 * P], ident32[:])
+        m4 = const.tile([P, 4], F32)
+        nc.vector.tensor_reduce(
+            out=m4[:], in_=ident32[:].rearrange("p (o v) -> p o v", o=4), axis=AX.X, op=ALU.add
+        )
+        bn_sel = const.tile([P, 2 * P], F32)
+        nc.vector.tensor_tensor(
+            out=bn_sel[:].rearrange("p (c o) -> p c o", o=4),
+            in0=rt[:].rearrange("p (c o) -> p c o", o=4),
+            in1=m4[:].unsqueeze(1).to_broadcast([P, 64, 4]),
+            op=ALU.mult,
+        )
+        scsh = const.tile([P, 64], F32)
+        nc.vector.tensor_reduce(
+            out=scsh[:], in_=bn_sel[:].rearrange("p (c o) -> p c o", o=4), axis=AX.X, op=ALU.add
+        )
+
+        raws = {}
+        state = {"next": 0, "pending": None}
+
+        def load_feat(g):
+            r = raw_pool.tile([P, 2048], BF16, tag="raw", name="raw_f")
+            for c in range(4):
+                nc.sync.dma_start(
+                    out=r[:, 512 * c : 512 * c + 512],
+                    in_=feat[:, 0, 4 * g + c].rearrange("s (q j) t -> s q (j t)", j=4),
+                )
+            raws[g] = r
+
+        def flush():
+            if state["pending"] is not None:
+                g, gt = state["pending"]
+                nc.vector.quantize_mx(
+                    out=f_codes[:, 512 * g : 512 * g + 512].bitcast(FP8X4),
+                    scales=f_scales[:, 512 * g : 512 * g + 512],
+                    in_=gt[:],
+                )
+                state["pending"] = None
+
+        def feat_step(engine):
+            g = state["next"]
+            if g >= N_TILES:
+                return
+            state["next"] = g + 1
+            if g + PREFETCH < N_TILES:
+                load_feat(g + PREFETCH)
+            gt = grp_pool.tile([P, 2048], BF16, tag="grp", name="grp_f", align_bytes=64)
+            regroup(gt[:], raws[g][:], 4, engine)
+            flush()
+            state["pending"] = (g, gt)
+
+        for g in range(PREFETCH):
+            load_feat(g)
+
+        in2 = big.tile([P, COUT * V * 4], BF16, tag="in2", name="in2", align_bytes=64)
+        in2_v = in2[:].rearrange("p (g v o j) -> p g v o j", g=32, v=V, o=4)
+        for h in range(2):
+            xh = big.tile([P, 8192], F32, tag="x", name="xh")
+            xh_v = xh[:].rearrange("o (v j s w) -> o v j s w", v=16, j=4, s=S)
+            for s in range(S):
+                acc = ps_m.tile([P, 512], F32, tag="mm1", name="acc")
+                nc.tensor.matmul_mx(
+                    out=acc[:],
+                    lhsT=w_codes[:, P * s : P * s + P].bitcast(FP8X4),
+                    lhsT_scale=w_scales[:, P * s : P * s + P],
+                    rhs=a_codes[:, 512 * h : 512 * h + 512].bitcast(FP8X4),
+                    rhs_scale=a_scales[:, 512 * h : 512 * h + 512],
+                    start=True,
+                    stop=True,
+                )
+                nc.scalar.activation(
+                    out=xh_v[:, :, :, s, :],
+                    in_=acc[:].rearrange("o (v w j) -> o v j w", v=16, j=4),
+                    func=ACT.Identity,
+                    bias=cst[:, 4 + s : 5 + s],
+                    scale=1.0,
+                )
+                if s in (2, 5, 8, 10, 13, 15):
+                    feat_step("v")
+            for vl in range(16):
+                v = 16 * h + vl
+                tp = ps_t.tile([P, 512], F32, tag="tp", name="tp")
+                for j in range(4):
+                    col = (4 * vl + j) * P
+                    nc.tensor.transpose(tp[:, P * j : P * j + P], xh[:, col : col + P], ident32[:])
+                nc.vector.tensor_tensor(
+                    out=in2_v[:, :, v, :, :],
+                    in0=tp[:].rearrange("p (j g o) -> p g o j", j=4, o=4),
+                    in1=pa_t[:, 4 * v : 4 * v + 4].unsqueeze(1).unsqueeze(1).to_broadcast([P, 32, 4, 4]),
+                    op=ALU.mult,
+                )
+                if vl in (3, 7, 11, 15):
+                    feat_step("s")
+
+        for c in range(4):
+            nc.vector.quantize_mx(
+                out=g_codes[:, 1024 * c : 1024 * c + 1024].bitcast(FP8X4),
+                scales=g_scales[:, 1024 * c : 1024 * c + 1024],
+                in_=in2[:, 4096 * c : 4096 * c + 4096],
+            )
+            if c in (0, 2):
+                feat_step("s")
+
+        res_t = big.tile([P, 32 * T], BF16, tag="in2", name="res_t", align_bytes=64)
+        nc.sync.dma_start(
+            out=res_t[:].rearrange("p (g t) -> p g t", g=32),
+            in_=res.rearrange("n o v t -> (n o v) t").rearrange("(g p) t -> p g t", p=P),
+        )
+        out_v = out.rearrange("n o v t -> (n o v) t").rearrange("(g p) t -> p g t", p=P)
+        late = big.tile([P, 8192], F32, tag="x", name="late")
+        tail_engines = ["v", "v", "s", "v", "v", "s", "v", "v", "s", "v"]
+        steps_before = [2, 1, 1, 1, 1, 1, 1, 2]
+        used = 0
+        for qd in range(8):
+            for i in range(steps_before[qd]):
+                feat_step(tail_engines[used])
+                used += 1
+            if state["pending"] is not None and state["pending"][0] <= 4 * qd + 3:
+                flush()
+            slot = 512 * (qd % 4)
+            yq = late[:, slot : slot + 512]
+            t1 = late[:, 2048 + slot : 2048 + slot + 512]
+            ot = late[:, 4096 + slot : 4096 + slot + 512]
+            for o in range(4):
+                s2 = ps_s.tile([P, 512], F32, tag="s2", name="s2")
+                for k in range(4):
+                    g = 4 * qd + k
+                    ch = 4 * g + o
+                    nc.tensor.matmul_mx(
+                        out=s2[:, P * k : P * k + P],
+                        lhsT=f_codes[:, P * ch : P * ch + P].bitcast(FP8X4),
+                        lhsT_scale=f_scales[:, P * ch : P * ch + P],
+                        rhs=g_codes[:, P * g : P * g + P].bitcast(FP8X4),
+                        rhs_scale=g_scales[:, P * g : P * g + P],
+                        start=True,
+                        stop=True,
+                    )
+                nc.scalar.copy(
+                    out=yq.rearrange("t (k o v) -> t k o v", k=4, o=4)[:, :, o, :],
+                    in_=s2[:].rearrange("t (k v o) -> t k v o", k=4, o=4)[:, :, :, o],
+                )
+            ft = ps_t.tile([P, 512], F32, tag="tp", name="ft")
+            for k in range(4):
+                nc.tensor.transpose(ft[:, P * k : P * k + P], yq[:, P * k : P * k + P], ident32[:])
+            for k in range(4):
+                g = 4 * qd + k
+                nc.vector.scalar_tensor_tensor(
+                    out=t1[:, P * k : P * k + P],
+                    in0=ft[:, P * k : P * k + P],
+                    scalar=scsh[:, g : g + 1],
+                    in1=res_t[:, T * g : T * g + T],
+                    op0=ALU.mult,
+                    op1=ALU.add,
+                )
+                nc.scalar.activation(
+                    out=ot[:, P * k : P * k + P],
+                    in_=t1[:, P * k : P * k + P],
+                    func=ACT.Relu,
+                    bias=scsh[:, 32 + g : 33 + g],
+                    scale=1.0,
+                )
+            nc.sync.dma_start(
+                out=out_v[:, 4 * qd : 4 * qd + 4, :],
+                in_=ot.rearrange("p (k t) -> p k t", k=4),
+            )

@@ -17,7 +17,12 @@ S, CIN, COUT, V, T = 16, 512, 128, 32, 128
 EPS = 1e-5
 FLOPS = 2 * S * COUT * CIN * V * V + 2 * COUT * V * S * V * T
 N_TILES = COUT // 4
-PREFETCH = 5
+RAW_BUFS = 6
+TILES_T0, TILES_S1, TILES_T1, TILES_QG = 7, 6, 5, 2
+
+
+def evenly(i, n, total):
+    return (i + 1) * n // total > i * n // total
 
 
 def tile_multiscale_gcn_pa_kernel(
@@ -28,11 +33,12 @@ def tile_multiscale_gcn_pa_kernel(
         const = ctx.enter_context(tc.tile_pool(name="const", bufs=1))
         keep = ctx.enter_context(tc.tile_pool(name="keep", bufs=1))
         big = ctx.enter_context(tc.tile_pool(name="big", bufs=1))
-        raw_pool = ctx.enter_context(tc.tile_pool(name="rawp", bufs=PREFETCH + 1))
+        raw_pool = ctx.enter_context(tc.tile_pool(name="rawp", bufs=RAW_BUFS))
         grp_pool = ctx.enter_context(tc.tile_pool(name="grpp", bufs=4))
-        ps_m = ctx.enter_context(tc.psum_pool(name="psm", bufs=2))
-        ps_t = ctx.enter_context(tc.psum_pool(name="pst", bufs=3))
-        ps_s = ctx.enter_context(tc.psum_pool(name="pss", bufs=3))
+        res_pool = ctx.enter_context(tc.tile_pool(name="resp", bufs=4))
+        ps_m = ctx.enter_context(tc.psum_pool(name="psm", bufs=4))
+        ps_t = ctx.enter_context(tc.psum_pool(name="pst", bufs=4))
+        ctx.enter_context(tc.manual_schedule())
 
         w_codes = keep.tile([P, S * COUT], U32, align_bytes=64)
         w_scales = keep.tile([P, S * COUT], U8, align_bytes=64)
@@ -43,49 +49,67 @@ def tile_multiscale_gcn_pa_kernel(
         f_codes = keep.tile([P, COUT * T], U32, align_bytes=64)
         f_scales = keep.tile([P, COUT * T], U8, align_bytes=64)
 
+        zrows = const.tile([P, P], BF16)
+        nc.vector.memset(zrows[:], 0.0)
+        sq = const.tile([P, 2], F32)
+        nc.vector.memset(sq[:], 1.0)
+        nc.scalar.sqrt(out=sq[:, 1:2], in_=sq[:, 0:1])
         ident32 = const.tile([P, P], F32)
         make_identity(nc, ident32[:])
         identb = const.tile([P, P], BF16)
         make_identity(nc, identb[:])
-        zrows = const.tile([P, P], BF16)
-        nc.vector.memset(zrows[:], 0.0)
-
-        a2 = ada_A.rearrange("n i v w -> (n i) (v w)")
-
-        def load_a(h):
-            r = raw_pool.tile([P, 2048], BF16, tag="raw", name="raw_a")
-            r3 = r[:].rearrange("q (t c) -> q t c", t=4)
-            for u in range(2):
-                nc.sync.dma_start(
-                    out=r3[:, 2 * u : 2 * u + 2, :],
-                    in_=a2[256 * u : 256 * u + 256, 512 * h : 512 * h + 512].rearrange(
-                        "(q e) c -> q e c", e=2
-                    ),
-                )
-            return r
-
-        def load_w(c):
-            r = raw_pool.tile([P, 2048], BF16, tag="raw", name="raw_w")
-            nc.sync.dma_start(
-                out=r[:].rearrange("o (s i) -> o s i", s=4),
-                in_=ada_w[4 * c : 4 * c + 4].rearrange("s o i -> o s i"),
-            )
-            return r
-
-        raw_a = [load_a(0)]
-        raw_w = [load_w(0), load_w(1)]
         nc.scalar.dma_start(out=zrows[4:20, :], in_=ada_b)
+        nc.scalar.dma_start(out=zrows[3:4, :], in_=bn_var.unsqueeze(0))
         nc.scalar.dma_start(out=zrows[0:1, :], in_=bn_gamma.unsqueeze(0))
         nc.scalar.dma_start(out=zrows[1:2, :], in_=bn_beta.unsqueeze(0))
         nc.scalar.dma_start(out=zrows[2:3, :], in_=bn_mean.unsqueeze(0))
-        nc.scalar.dma_start(out=zrows[3:4, :], in_=bn_var.unsqueeze(0))
-        raw_w.append(load_w(2))
-        raw_w.append(load_w(3))
-        raw_a.append(load_a(1))
+
+        a2 = ada_A.rearrange("n i v w -> (n i) (v w)")
+        raws = {}
+
+        def load(kind, n):
+            r = raw_pool.tile([P, 2048], BF16, tag="raw", name="raw")
+            raws[(kind, n)] = r
+            if kind == "a":
+                r3 = r[:].rearrange("q (t c) -> q t c", t=4)
+                for u in range(2):
+                    nc.sync.dma_start(
+                        out=r3[:, 2 * u : 2 * u + 2, :],
+                        in_=a2[256 * u : 256 * u + 256, 512 * n : 512 * n + 512].rearrange(
+                            "(q e) c -> q e c", e=2
+                        ),
+                    )
+            elif kind == "w":
+                nc.sync.dma_start(
+                    out=r[:].rearrange("o (s i) -> o s i", s=4),
+                    in_=ada_w[4 * n : 4 * n + 4].rearrange("s o i -> o s i"),
+                )
+            else:
+                for c in range(4):
+                    nc.sync.dma_start(
+                        out=r[:, 512 * c : 512 * c + 512],
+                        in_=feat[:, 0, 4 * n + c].rearrange("s (q j) t -> s q (j t)", j=4),
+                    )
+
+        loads = [("a", 0), ("w", 0), ("w", 1), ("w", 2), ("f", 0), ("w", 3), ("f", 1), ("a", 1)]
+        loads.extend([("f", g) for g in range(2, N_TILES)])
+        state = {"loaded": 0, "next": 0, "quantised": 0}
+
+        def load_next():
+            if state["loaded"] < len(loads):
+                kind, n = loads[state["loaded"]]
+                state["loaded"] += 1
+                load(kind, n)
+
+        for i in range(3):
+            load_next()
         pa_full = const.tile([P, V * V], BF16)
-        pa_rows = PA.rearrange("s v w -> s (v w)")
-        for q in range(8):
-            nc.scalar.dma_start(out=pa_full[q:P:8, :], in_=pa_rows)
+        nc.sync.dma_start(
+            out=pa_full[:],
+            in_=PA.rearrange("s v w -> s (v w)").unsqueeze(1).to_broadcast([S, 8, V * V]),
+        )
+        for i in range(RAW_BUFS - 3):
+            load_next()
 
         def regroup(dst, src, n, engine):
             if engine == "v":
@@ -107,31 +131,34 @@ def tile_multiscale_gcn_pa_kernel(
                         in_=src[:, w * b : w * b + w].rearrange("p (t c i) -> p c t i", t=4, i=4),
                     )
 
-        zt = ps_t.tile([P, P], BF16, tag="tp", name="zt")
-        nc.tensor.transpose(zt[:], zrows[:], identb[:])
-        cst = const.tile([P, 20], F32)
-        nc.vector.tensor_copy(out=cst[:], in_=zt[:, 0:20])
-
-        def quant_a(h):
-            g = grp_pool.tile([P, 2048], BF16, tag="grp", name="grp_a", align_bytes=64)
-            regroup(g[:], raw_a[h][:], 1, "v")
-            return g
-
-        def quant_a2(h, g):
+        def quantise(codes, scales, c0, width, src):
             nc.vector.quantize_mx(
-                out=a_codes[:, 512 * h : 512 * h + 512].bitcast(FP8X4),
-                scales=a_scales[:, 512 * h : 512 * h + 512],
-                in_=g[:],
+                out=codes[:, c0 : c0 + width].bitcast(FP8X4), scales=scales[:, c0 : c0 + width], in_=src
             )
 
-        ga0 = quant_a(0)
+        m8 = const.tile([P, 8], F32)
+        nc.vector.tensor_reduce(
+            out=m8[:], in_=ident32[:].rearrange("p (s w) -> p w s", w=8), axis=AX.X, op=ALU.add
+        )
+        m4 = const.tile([P, 4], F32)
+        nc.vector.tensor_reduce(
+            out=m4[:], in_=ident32[:].rearrange("p (o v) -> p o v", o=4), axis=AX.X, op=ALU.add
+        )
+
+        grp_a0 = grp_pool.tile([P, 2048], BF16, tag="grp", name="grp_a0", align_bytes=64)
+        regroup(grp_a0[:], raws[("a", 0)][:], 1, "v")
+        load_next()
+
+        quantise(a_codes, a_scales, 0, 512, grp_a0[:])
 
         def w_transposes(c):
-            r32 = raw_w[c][:].bitcast(F32)
+            r32 = raws[("w", c)][:].bitcast(F32)
             g = grp_pool.tile([P, 2048], BF16, tag="grp", name="grp_w", align_bytes=64)
             g32 = g[:].bitcast(F32)
+            banks = []
             for a in range(2):
                 wt = ps_t.tile([P, 512], F32, tag="tp", name="wt")
+                banks.append(wt)
                 for b in range(2):
                     for u in range(2):
                         col = (2 * a + b) * 256 + u * 128
@@ -140,139 +167,60 @@ def tile_multiscale_gcn_pa_kernel(
                             r32[:, col : col + 128],
                             ident32[:],
                         )
-                nc.scalar.copy(
-                    out=g32[:, 512 * a : 512 * a + 512].rearrange("q (b o u) -> q b o u", b=2, u=2),
-                    in_=wt[:].rearrange("q (b u o) -> q b o u", b=2, u=2),
-                )
+            for a in range(2):
+                dst = g32[:, 512 * a : 512 * a + 512].rearrange("q (b o u) -> q b o u", b=2, u=2)
+                src = banks[a][:].rearrange("q (b u o) -> q b o u", b=2, u=2)
+                if a == 0:
+                    nc.scalar.copy(out=dst, in_=src)
+                else:
+                    nc.vector.tensor_copy(out=dst, in_=src)
+            load_next()
             return g
 
-        def w_quant(c, g):
-            nc.vector.quantize_mx(
-                out=w_codes[:, 512 * c : 512 * c + 512].bitcast(FP8X4),
-                scales=w_scales[:, 512 * c : 512 * c + 512],
-                in_=g[:],
-            )
+        grouped = {}
 
-        gw0 = w_transposes(0)
-        quant_a2(0, ga0)
-        gw1 = w_transposes(1)
-        w_quant(0, gw0)
-        gw2 = w_transposes(2)
-        w_quant(1, gw1)
-        gw3 = w_transposes(3)
-        w_quant(2, gw2)
-        ga1 = quant_a(1)
-        w_quant(3, gw3)
-        quant_a2(1, ga1)
-
-        m8 = const.tile([P, 8], F32)
-        nc.vector.tensor_reduce(
-            out=m8[:], in_=ident32[:].rearrange("p (s w) -> p w s", w=8), axis=AX.X, op=ALU.add
-        )
-        pa_sel = const.tile([P, V * V], F32)
-        nc.vector.tensor_tensor(
-            out=pa_sel[:].rearrange("p (v j w) -> p v j w", v=V, j=4),
-            in0=pa_full[:].rearrange("p (v w j) -> p v j w", v=V, j=4),
-            in1=m8[:].unsqueeze(1).unsqueeze(1).to_broadcast([P, V, 4, 8]),
-            op=ALU.mult,
-        )
-        pa_t = const.tile([P, V * 4], F32)
-        nc.vector.tensor_reduce(
-            out=pa_t[:], in_=pa_sel[:].rearrange("p (c w) -> p c w", w=8), axis=AX.X, op=ALU.add
-        )
-
-        bn = const.tile([P, 8], F32)
-        nc.vector.tensor_scalar_add(out=bn[:, 0:1], in0=cst[:, 3:4], scalar1=EPS)
-        sq = const.tile([P, 1], F32)
-        nc.scalar.sqrt(out=sq[:], in_=bn[:, 0:1])
-        nc.vector.reciprocal(out=bn[:, 1:2], in_=sq[:])
-        nc.vector.tensor_tensor(out=bn[:, 2:3], in0=cst[:, 0:1], in1=bn[:, 1:2], op=ALU.mult)
-        nc.vector.tensor_tensor(out=bn[:, 3:4], in0=cst[:, 2:3], in1=bn[:, 2:3], op=ALU.mult)
-        nc.vector.tensor_tensor(out=bn[:, 4:5], in0=cst[:, 1:2], in1=bn[:, 3:4], op=ALU.subtract)
-        rep = const.tile([P, 2 * P], F32)
-        nc.vector.tensor_copy(out=rep[:, 0:P], in_=bn[:, 2:3].to_broadcast([P, P]))
-        nc.vector.tensor_copy(out=rep[:, P : 2 * P], in_=bn[:, 4:5].to_broadcast([P, P]))
-        rt = ps_t.tile([P, 2 * P], F32, tag="tp", name="rt")
-        nc.tensor.transpose(rt[:, 0:P], rep[:, 0:P], ident32[:])
-        nc.tensor.transpose(rt[:, P : 2 * P], rep[:, P : 2 * P], ident32[:])
-        m4 = const.tile([P, 4], F32)
-        nc.vector.tensor_reduce(
-            out=m4[:], in_=ident32[:].rearrange("p (o v) -> p o v", o=4), axis=AX.X, op=ALU.add
-        )
-        bn_sel = const.tile([P, 2 * P], F32)
-        nc.vector.tensor_tensor(
-            out=bn_sel[:].rearrange("p (c o) -> p c o", o=4),
-            in0=rt[:].rearrange("p (c o) -> p c o", o=4),
-            in1=m4[:].unsqueeze(1).to_broadcast([P, 64, 4]),
-            op=ALU.mult,
-        )
-        scsh = const.tile([P, 64], F32)
-        nc.vector.tensor_reduce(
-            out=scsh[:], in_=bn_sel[:].rearrange("p (c o) -> p c o", o=4), axis=AX.X, op=ALU.add
-        )
-
-        raws = {}
-        state = {"next": 0, "pending": None}
-
-        def load_feat(g):
-            r = raw_pool.tile([P, 2048], BF16, tag="raw", name="raw_f")
-            for c in range(4):
-                nc.sync.dma_start(
-                    out=r[:, 512 * c : 512 * c + 512],
-                    in_=feat[:, 0, 4 * g + c].rearrange("s (q j) t -> s q (j t)", j=4),
-                )
-            raws[g] = r
-
-        def flush():
-            if state["pending"] is not None:
-                g, gt = state["pending"]
-                nc.vector.quantize_mx(
-                    out=f_codes[:, 512 * g : 512 * g + 512].bitcast(FP8X4),
-                    scales=f_scales[:, 512 * g : 512 * g + 512],
-                    in_=gt[:],
-                )
-                state["pending"] = None
+        def quantise_oldest():
+            g = state["quantised"]
+            state["quantised"] = g + 1
+            quantise(f_codes, f_scales, 512 * g, 512, grouped[g][:])
 
         def feat_step(engine):
             g = state["next"]
-            if g >= N_TILES:
-                return
             state["next"] = g + 1
-            if g + PREFETCH < N_TILES:
-                load_feat(g + PREFETCH)
             gt = grp_pool.tile([P, 2048], BF16, tag="grp", name="grp_f", align_bytes=64)
-            regroup(gt[:], raws[g][:], 4, engine)
-            flush()
-            state["pending"] = (g, gt)
+            regroup(gt[:], raws[("f", g)][:], 4, engine)
+            load_next()
+            grouped[g] = gt
+            while state["quantised"] < g:
+                quantise_oldest()
 
-        for g in range(PREFETCH):
-            load_feat(g)
+        def first_pass(h, s):
+            acc = ps_m.tile([P, 512], F32, tag="mm", name="acc")
+            nc.tensor.matmul_mx(
+                out=acc[:],
+                lhsT=w_codes[:, P * s : P * s + P].bitcast(FP8X4),
+                lhsT_scale=w_scales[:, P * s : P * s + P],
+                rhs=a_codes[:, 512 * h : 512 * h + 512].bitcast(FP8X4),
+                rhs_scale=a_scales[:, 512 * h : 512 * h + 512],
+                start=True,
+                stop=True,
+            )
+            return acc
+
+        def add_bias(xh, s, acc):
+            nc.scalar.activation(
+                out=xh[:].rearrange("o (v j s w) -> o v j s w", v=16, j=4, s=S)[:, :, :, s, :],
+                in_=acc[:].rearrange("o (v w j) -> o v j w", v=16, j=4),
+                func=ACT.Identity,
+                bias=cst[:, 4 + s : 5 + s],
+                scale=1.0,
+            )
 
         in2 = big.tile([P, COUT * V * 4], BF16, tag="in2", name="in2", align_bytes=64)
         in2_v = in2[:].rearrange("p (g v o j) -> p g v o j", g=32, v=V, o=4)
-        for h in range(2):
-            xh = big.tile([P, 8192], F32, tag="x", name="xh")
-            xh_v = xh[:].rearrange("o (v j s w) -> o v j s w", v=16, j=4, s=S)
-            for s in range(S):
-                acc = ps_m.tile([P, 512], F32, tag="mm1", name="acc")
-                nc.tensor.matmul_mx(
-                    out=acc[:],
-                    lhsT=w_codes[:, P * s : P * s + P].bitcast(FP8X4),
-                    lhsT_scale=w_scales[:, P * s : P * s + P],
-                    rhs=a_codes[:, 512 * h : 512 * h + 512].bitcast(FP8X4),
-                    rhs_scale=a_scales[:, 512 * h : 512 * h + 512],
-                    start=True,
-                    stop=True,
-                )
-                nc.scalar.activation(
-                    out=xh_v[:, :, :, s, :],
-                    in_=acc[:].rearrange("o (v w j) -> o v j w", v=16, j=4),
-                    func=ACT.Identity,
-                    bias=cst[:, 4 + s : 5 + s],
-                    scale=1.0,
-                )
-                if s in (2, 5, 8, 10, 13, 15):
-                    feat_step("v")
+        pa_t = const.tile([P, V * 4], F32)
+
+        def transposes_and_pa(h, xh, n_tiles):
             for vl in range(16):
                 v = 16 * h + vl
                 tp = ps_t.tile([P, 512], F32, tag="tp", name="tp")
@@ -285,45 +233,109 @@ def tile_multiscale_gcn_pa_kernel(
                     in1=pa_t[:, 4 * v : 4 * v + 4].unsqueeze(1).unsqueeze(1).to_broadcast([P, 32, 4, 4]),
                     op=ALU.mult,
                 )
-                if vl in (3, 7, 11, 15):
+                if evenly(vl, n_tiles, 16):
                     feat_step("s")
 
+        x0 = big.tile([P, 8192], F32, tag="x", name="x0")
+        grp_w = w_transposes(0)
+        quantise(w_codes, w_scales, 0, 512, grp_w[:])
+        zt = ps_t.tile([P, P], BF16, tag="tp", name="zt")
+        nc.tensor.transpose(zt[:], zrows[:], identb[:])
+        cst = const.tile([P, 20], F32)
+        nc.vector.tensor_copy(out=cst[:], in_=zt[:, 0:20])
+        bn = const.tile([P, 8], F32)
+        nc.vector.tensor_scalar_add(out=bn[:, 0:1], in0=cst[:, 3:4], scalar1=EPS)
+        rep = const.tile([P, 2 * P], F32)
+        scsh = const.tile([P, 64], F32)
         for c in range(4):
-            nc.vector.quantize_mx(
-                out=g_codes[:, 1024 * c : 1024 * c + 1024].bitcast(FP8X4),
-                scales=g_scales[:, 1024 * c : 1024 * c + 1024],
-                in_=in2[:, 4096 * c : 4096 * c + 4096],
-            )
-            if c in (0, 2):
+            if c < 3:
+                grp_w = w_transposes(c + 1)
+            if c == 2:
+                rt = ps_t.tile([P, 2 * P], F32, tag="tp", name="rt")
+                nc.tensor.transpose(rt[:, 0:P], rep[:, 0:P], ident32[:])
+                nc.tensor.transpose(rt[:, P : 2 * P], rep[:, P : 2 * P], ident32[:])
+            accs = [first_pass(0, s) for s in range(4 * c, 4 * c + 4)]
+            if c == 1:
+                nc.vector.reciprocal(out=bn[:, 1:2], in_=sq[:, 1:2])
+                nc.vector.tensor_tensor(out=bn[:, 2:3], in0=cst[:, 0:1], in1=bn[:, 1:2], op=ALU.mult)
+                nc.vector.tensor_tensor(out=bn[:, 3:4], in0=cst[:, 2:3], in1=bn[:, 2:3], op=ALU.mult)
+                nc.vector.tensor_tensor(out=bn[:, 4:5], in0=cst[:, 1:2], in1=bn[:, 3:4], op=ALU.subtract)
+                nc.vector.tensor_copy(out=rep[:, 0:P], in_=bn[:, 2:3].to_broadcast([P, P]))
+                nc.vector.tensor_copy(out=rep[:, P : 2 * P], in_=bn[:, 4:5].to_broadcast([P, P]))
+            if c == 3:
+                bn_sel = const.tile([P, 2 * P], F32)
+                nc.vector.tensor_tensor(
+                    out=bn_sel[:].rearrange("p (c o) -> p c o", o=4),
+                    in0=rt[:].rearrange("p (c o) -> p c o", o=4),
+                    in1=m4[:].unsqueeze(1).to_broadcast([P, 64, 4]),
+                    op=ALU.mult,
+                )
+                nc.vector.tensor_reduce(
+                    out=scsh[:], in_=bn_sel[:].rearrange("p (c o) -> p c o", o=4), axis=AX.X, op=ALU.add
+                )
+            if c == 0:
+                pa_sel = const.tile([P, V * V], F32)
+                nc.vector.tensor_tensor(
+                    out=pa_sel[:].rearrange("p (v j w) -> p v j w", v=V, j=4),
+                    in0=pa_full[:].rearrange("p (v w j) -> p v j w", v=V, j=4),
+                    in1=m8[:].unsqueeze(1).unsqueeze(1).to_broadcast([P, V, 4, 8]),
+                    op=ALU.mult,
+                )
+                nc.vector.tensor_reduce(
+                    out=pa_t[:], in_=pa_sel[:].rearrange("p (c w) -> p c w", w=8), axis=AX.X, op=ALU.add
+                )
+            if c < 3:
+                quantise(w_codes, w_scales, 512 * (c + 1), 512, grp_w[:])
+            for s in range(4 * c, 4 * c + 4):
+                add_bias(x0, s, accs[s - 4 * c])
+            if c == 0:
+                nc.scalar.sqrt(out=sq[:, 1:2], in_=bn[:, 0:1])
+            if c == 3:
+                grp_a1 = grp_pool.tile([P, 2048], BF16, tag="grp", name="grp_a1", align_bytes=64)
+                regroup(grp_a1[:], raws[("a", 1)][:], 1, "v")
+                load_next()
+            if c > 0:
+                feat_step("v")
+        quantise(a_codes, a_scales, 512, 512, grp_a1[:])
+        transposes_and_pa(0, x0, TILES_T0)
+        x1 = big.tile([P, 8192], F32, tag="x", name="x1")
+        for s in range(S):
+            add_bias(x1, s, first_pass(1, s))
+            if evenly(s, TILES_S1, S):
+                feat_step("v")
+        transposes_and_pa(1, x1, TILES_T1)
+        for c in range(4):
+            quantise(g_codes, g_scales, 1024 * c, 1024, in2[:, 4096 * c : 4096 * c + 4096])
+            if evenly(c, TILES_QG, 4):
                 feat_step("s")
 
-        res_t = big.tile([P, 32 * T], BF16, tag="in2", name="res_t", align_bytes=64)
-        nc.sync.dma_start(
-            out=res_t[:].rearrange("p (g t) -> p g t", g=32),
-            in_=res.rearrange("n o v t -> (n o v) t").rearrange("(g p) t -> p g t", p=P),
-        )
+        res_v = res.rearrange("n o v t -> (n o v) t").rearrange("(g p) t -> p g t", p=P)
         out_v = out.rearrange("n o v t -> (n o v) t").rearrange("(g p) t -> p g t", p=P)
         late = big.tile([P, 8192], F32, tag="x", name="late")
-        tail_engines = ["v", "v", "s", "v", "v", "s", "v", "v", "s", "v"]
-        steps_before = [2, 1, 1, 1, 1, 1, 1, 2]
-        used = 0
-        for qd in range(8):
-            for i in range(steps_before[qd]):
-                feat_step(tail_engines[used])
-                used += 1
-            if state["pending"] is not None and state["pending"][0] <= 4 * qd + 3:
-                flush()
-            slot = 512 * (qd % 4)
-            yq = late[:, slot : slot + 512]
-            t1 = late[:, 2048 + slot : 2048 + slot + 512]
-            ot = late[:, 4096 + slot : 4096 + slot + 512]
-            for o in range(4):
-                s2 = ps_s.tile([P, 512], F32, tag="s2", name="s2")
-                for k in range(4):
-                    g = 4 * qd + k
+        res_tiles = {}
+
+        def load_res(qd):
+            if qd < 8:
+                r = res_pool.tile([P, 4 * T], BF16, tag="res", name="res_t")
+                nc.sync.dma_start(
+                    out=r[:].rearrange("p (g t) -> p g t", g=4), in_=res_v[:, 4 * qd : 4 * qd + 4, :]
+                )
+                res_tiles[qd] = r
+
+        def part(kind, qd):
+            c0 = 2048 * kind + 512 * (qd % 3)
+            return late[:, c0 : c0 + 512]
+
+        def second_passes(qd):
+            while state["quantised"] < 4 * qd + 4:
+                quantise_oldest()
+            banks = [ps_m.tile([P, 512], F32, tag="mm", name="s2") for o in range(4)]
+            for k in range(4):
+                g = 4 * qd + k
+                for o in range(4):
                     ch = 4 * g + o
                     nc.tensor.matmul_mx(
-                        out=s2[:, P * k : P * k + P],
+                        out=banks[o][:, P * k : P * k + P],
                         lhsT=f_codes[:, P * ch : P * ch + P].bitcast(FP8X4),
                         lhsT_scale=f_scales[:, P * ch : P * ch + P],
                         rhs=g_codes[:, P * g : P * g + P].bitcast(FP8X4),
@@ -331,31 +343,56 @@ def tile_multiscale_gcn_pa_kernel(
                         start=True,
                         stop=True,
                     )
+            for o in range(4):
                 nc.scalar.copy(
-                    out=yq.rearrange("t (k o v) -> t k o v", k=4, o=4)[:, :, o, :],
-                    in_=s2[:].rearrange("t (k v o) -> t k v o", k=4, o=4)[:, :, :, o],
+                    out=part(0, qd).rearrange("t (k o v) -> t k o v", k=4, o=4)[:, :, o, :],
+                    in_=banks[o][:].rearrange("t (k v o) -> t k v o", k=4, o=4)[:, :, :, o],
                 )
+
+        def back_and_norm(qd):
             ft = ps_t.tile([P, 512], F32, tag="tp", name="ft")
             for k in range(4):
-                nc.tensor.transpose(ft[:, P * k : P * k + P], yq[:, P * k : P * k + P], ident32[:])
+                nc.tensor.transpose(
+                    ft[:, P * k : P * k + P], part(0, qd)[:, P * k : P * k + P], ident32[:]
+                )
             for k in range(4):
                 g = 4 * qd + k
                 nc.vector.scalar_tensor_tensor(
-                    out=t1[:, P * k : P * k + P],
+                    out=part(1, qd)[:, P * k : P * k + P],
                     in0=ft[:, P * k : P * k + P],
                     scalar=scsh[:, g : g + 1],
-                    in1=res_t[:, T * g : T * g + T],
+                    in1=res_tiles[qd][:, T * k : T * k + T],
                     op0=ALU.mult,
                     op1=ALU.add,
                 )
+
+        def relu_and_store(qd):
+            for k in range(4):
+                g = 4 * qd + k
                 nc.scalar.activation(
-                    out=ot[:, P * k : P * k + P],
-                    in_=t1[:, P * k : P * k + P],
+                    out=part(2, qd)[:, P * k : P * k + P],
+                    in_=part(1, qd)[:, P * k : P * k + P],
                     func=ACT.Relu,
                     bias=scsh[:, 32 + g : 33 + g],
                     scale=1.0,
                 )
             nc.sync.dma_start(
                 out=out_v[:, 4 * qd : 4 * qd + 4, :],
-                in_=ot.rearrange("p (k t) -> p k t", k=4),
+                in_=part(2, qd).rearrange("p (k t) -> p k t", k=4),
             )
+
+        load_res(0)
+        load_res(1)
+        first_left = state["next"]
+        left = N_TILES - first_left
+        for i in range(10):
+            if i < 8:
+                want = max(4 * i + 4, first_left + ((i + 1) * left + 7) // 8)
+                while state["next"] < want:
+                    feat_step("s" if (state["next"] - first_left) % 2 == 1 else "v")
+                load_res(i + 2)
+                second_passes(i)
+            if 1 <= i <= 8:
+                back_and_norm(i - 1)
+            if i >= 2:
+                relu_and_store(i - 2)

@@ -18,7 +18,7 @@ EPS = 1e-5
 FLOPS = 2 * S * COUT * CIN * V * V + 2 * COUT * V * S * V * T
 N_TILES = COUT // 4
 RAW_BUFS = 6
-TILES_T0, TILES_S1, TILES_T1, TILES_QG = 7, 6, 5, 2
+TILES_T0, TILES_S1, TILES_T1, TILES_QG = 7, 6, 6, 3
 
 
 def evenly(i, n, total):
@@ -246,7 +246,8 @@ def tile_multiscale_gcn_pa_kernel(
         bn = const.tile([P, 8], F32)
         nc.vector.tensor_scalar_add(out=bn[:, 0:1], in0=cst[:, 3:4], scalar1=EPS)
         rep = const.tile([P, 2 * P], F32)
-        scsh = const.tile([P, 64], F32)
+        scale_row = const.tile([P, P], F32)
+        shift = const.tile([P, 32], F32)
         for c in range(4):
             if c < 3:
                 grp_w = w_transposes(c + 1)
@@ -263,15 +264,16 @@ def tile_multiscale_gcn_pa_kernel(
                 nc.vector.tensor_copy(out=rep[:, 0:P], in_=bn[:, 2:3].to_broadcast([P, P]))
                 nc.vector.tensor_copy(out=rep[:, P : 2 * P], in_=bn[:, 4:5].to_broadcast([P, P]))
             if c == 3:
-                bn_sel = const.tile([P, 2 * P], F32)
+                nc.vector.tensor_copy(out=scale_row[:], in_=rt[:, 0:P])
+                bn_sel = const.tile([P, P], F32)
                 nc.vector.tensor_tensor(
                     out=bn_sel[:].rearrange("p (c o) -> p c o", o=4),
-                    in0=rt[:].rearrange("p (c o) -> p c o", o=4),
-                    in1=m4[:].unsqueeze(1).to_broadcast([P, 64, 4]),
+                    in0=rt[:, P : 2 * P].rearrange("p (c o) -> p c o", o=4),
+                    in1=m4[:].unsqueeze(1).to_broadcast([P, 32, 4]),
                     op=ALU.mult,
                 )
                 nc.vector.tensor_reduce(
-                    out=scsh[:], in_=bn_sel[:].rearrange("p (c o) -> p c o", o=4), axis=AX.X, op=ALU.add
+                    out=shift[:], in_=bn_sel[:].rearrange("p (c o) -> p c o", o=4), axis=AX.X, op=ALU.add
                 )
             if c == 0:
                 pa_sel = const.tile([P, V * V], F32)
@@ -344,26 +346,30 @@ def tile_multiscale_gcn_pa_kernel(
                         stop=True,
                     )
             for o in range(4):
-                nc.scalar.copy(
+                nc.vector.tensor_tensor(
                     out=part(0, qd).rearrange("t (k o v) -> t k o v", k=4, o=4)[:, :, o, :],
-                    in_=banks[o][:].rearrange("t (k v o) -> t k v o", k=4, o=4)[:, :, :, o],
+                    in0=banks[o][:].rearrange("t (k v o) -> t k v o", k=4, o=4)[:, :, :, o],
+                    in1=scale_row[:, 16 * qd + o : 16 * qd + 16 : 4].unsqueeze(2).to_broadcast([P, 4, V]),
+                    op=ALU.mult,
                 )
 
-        def back_and_norm(qd):
+        back = {}
+
+        def back_and_residual(qd):
             ft = ps_t.tile([P, 512], F32, tag="tp", name="ft")
+            back[qd] = ft
             for k in range(4):
-                nc.tensor.transpose(
-                    ft[:, P * k : P * k + P], part(0, qd)[:, P * k : P * k + P], ident32[:]
+                cols = slice(P * k, P * k + P)
+                nc.tensor.matmul(
+                    out=ft[:, cols], lhsT=identb[:], rhs=res_tiles[qd][:, cols], start=True, stop=False
                 )
-            for k in range(4):
-                g = 4 * qd + k
-                nc.vector.scalar_tensor_tensor(
-                    out=part(1, qd)[:, P * k : P * k + P],
-                    in0=ft[:, P * k : P * k + P],
-                    scalar=scsh[:, g : g + 1],
-                    in1=res_tiles[qd][:, T * k : T * k + T],
-                    op0=ALU.mult,
-                    op1=ALU.add,
+                nc.tensor.matmul(
+                    out=ft[:, cols],
+                    lhsT=part(0, qd)[:, cols],
+                    rhs=ident32[:],
+                    is_transpose=True,
+                    start=False,
+                    stop=True,
                 )
 
         def relu_and_store(qd):
@@ -371,9 +377,9 @@ def tile_multiscale_gcn_pa_kernel(
                 g = 4 * qd + k
                 nc.scalar.activation(
                     out=part(2, qd)[:, P * k : P * k + P],
-                    in_=part(1, qd)[:, P * k : P * k + P],
+                    in_=back[qd][:, P * k : P * k + P],
                     func=ACT.Relu,
-                    bias=scsh[:, 32 + g : 33 + g],
+                    bias=shift[:, g : g + 1],
                     scale=1.0,
                 )
             nc.sync.dma_start(
@@ -393,6 +399,6 @@ def tile_multiscale_gcn_pa_kernel(
                 load_res(i + 2)
                 second_passes(i)
             if 1 <= i <= 8:
-                back_and_norm(i - 1)
+                back_and_residual(i - 1)
             if i >= 2:
                 relu_and_store(i - 2)

@@ -18,7 +18,7 @@ EPS = 1e-5
 FLOPS = 2 * S * COUT * CIN * V * V + 2 * COUT * V * S * V * T
 N_TILES = COUT // 4
 RAW_BUFS = 6
-TILES_T0, TILES_S1, TILES_T1, TILES_QG = 7, 6, 6, 3
+TILES_T0, TILES_S1, TILES_T1, TILES_QG = 8, 6, 5, 2
 
 
 def evenly(i, n, total):
@@ -246,8 +246,7 @@ def tile_multiscale_gcn_pa_kernel(
         bn = const.tile([P, 8], F32)
         nc.vector.tensor_scalar_add(out=bn[:, 0:1], in0=cst[:, 3:4], scalar1=EPS)
         rep = const.tile([P, 2 * P], F32)
-        scale_row = const.tile([P, P], F32)
-        shift = const.tile([P, 32], F32)
+        scsh = const.tile([P, 64], F32)
         for c in range(4):
             if c < 3:
                 grp_w = w_transposes(c + 1)
@@ -264,16 +263,15 @@ def tile_multiscale_gcn_pa_kernel(
                 nc.vector.tensor_copy(out=rep[:, 0:P], in_=bn[:, 2:3].to_broadcast([P, P]))
                 nc.vector.tensor_copy(out=rep[:, P : 2 * P], in_=bn[:, 4:5].to_broadcast([P, P]))
             if c == 3:
-                nc.vector.tensor_copy(out=scale_row[:], in_=rt[:, 0:P])
-                bn_sel = const.tile([P, P], F32)
+                bn_sel = const.tile([P, 2 * P], F32)
                 nc.vector.tensor_tensor(
                     out=bn_sel[:].rearrange("p (c o) -> p c o", o=4),
-                    in0=rt[:, P : 2 * P].rearrange("p (c o) -> p c o", o=4),
-                    in1=m4[:].unsqueeze(1).to_broadcast([P, 32, 4]),
+                    in0=rt[:].rearrange("p (c o) -> p c o", o=4),
+                    in1=m4[:].unsqueeze(1).to_broadcast([P, 64, 4]),
                     op=ALU.mult,
                 )
                 nc.vector.tensor_reduce(
-                    out=shift[:], in_=bn_sel[:].rearrange("p (c o) -> p c o", o=4), axis=AX.X, op=ALU.add
+                    out=scsh[:], in_=bn_sel[:].rearrange("p (c o) -> p c o", o=4), axis=AX.X, op=ALU.add
                 )
             if c == 0:
                 pa_sel = const.tile([P, V * V], F32)
@@ -297,6 +295,8 @@ def tile_multiscale_gcn_pa_kernel(
                 regroup(grp_a1[:], raws[("a", 1)][:], 1, "v")
                 load_next()
             if c > 0:
+                feat_step("v")
+            if c == 3:
                 feat_step("v")
         quantise(a_codes, a_scales, 512, 512, grp_a1[:])
         transposes_and_pa(0, x0, TILES_T0)
@@ -346,30 +346,26 @@ def tile_multiscale_gcn_pa_kernel(
                         stop=True,
                     )
             for o in range(4):
-                nc.vector.tensor_tensor(
+                nc.scalar.copy(
                     out=part(0, qd).rearrange("t (k o v) -> t k o v", k=4, o=4)[:, :, o, :],
-                    in0=banks[o][:].rearrange("t (k v o) -> t k v o", k=4, o=4)[:, :, :, o],
-                    in1=scale_row[:, 16 * qd + o : 16 * qd + 16 : 4].unsqueeze(2).to_broadcast([P, 4, V]),
-                    op=ALU.mult,
+                    in_=banks[o][:].rearrange("t (k v o) -> t k v o", k=4, o=4)[:, :, :, o],
                 )
 
-        back = {}
-
-        def back_and_residual(qd):
+        def back_and_norm(qd):
             ft = ps_t.tile([P, 512], F32, tag="tp", name="ft")
-            back[qd] = ft
             for k in range(4):
-                cols = slice(P * k, P * k + P)
-                nc.tensor.matmul(
-                    out=ft[:, cols], lhsT=identb[:], rhs=res_tiles[qd][:, cols], start=True, stop=False
+                nc.tensor.transpose(
+                    ft[:, P * k : P * k + P], part(0, qd)[:, P * k : P * k + P], ident32[:]
                 )
-                nc.tensor.matmul(
-                    out=ft[:, cols],
-                    lhsT=part(0, qd)[:, cols],
-                    rhs=ident32[:],
-                    is_transpose=True,
-                    start=False,
-                    stop=True,
+            for k in range(4):
+                g = 4 * qd + k
+                nc.vector.scalar_tensor_tensor(
+                    out=part(1, qd)[:, P * k : P * k + P],
+                    in0=ft[:, P * k : P * k + P],
+                    scalar=scsh[:, g : g + 1],
+                    in1=res_tiles[qd][:, T * k : T * k + T],
+                    op0=ALU.mult,
+                    op1=ALU.add,
                 )
 
         def relu_and_store(qd):
@@ -377,9 +373,9 @@ def tile_multiscale_gcn_pa_kernel(
                 g = 4 * qd + k
                 nc.scalar.activation(
                     out=part(2, qd)[:, P * k : P * k + P],
-                    in_=back[qd][:, P * k : P * k + P],
+                    in_=part(1, qd)[:, P * k : P * k + P],
                     func=ACT.Relu,
-                    bias=shift[:, g : g + 1],
+                    bias=scsh[:, 32 + g : 33 + g],
                     scale=1.0,
                 )
             nc.sync.dma_start(
@@ -395,10 +391,10 @@ def tile_multiscale_gcn_pa_kernel(
             if i < 8:
                 want = max(4 * i + 4, first_left + ((i + 1) * left + 7) // 8)
                 while state["next"] < want:
-                    feat_step("s" if (state["next"] - first_left) % 2 == 1 else "v")
+                    feat_step("s" if (state["next"] - first_left) % 3 == 2 else "v")
                 load_res(i + 2)
                 second_passes(i)
             if 1 <= i <= 8:
-                back_and_residual(i - 1)
+                back_and_norm(i - 1)
             if i >= 2:
                 relu_and_store(i - 2)

from contextlib import ExitStack

import concourse.mybir as mybir
from concourse.masks import make_identity

F32 = mybir.dt.float32
BF16 = mybir.dt.bfloat16
U32 = mybir.dt.uint32
U8 = mybir.dt.uint8
FP8X4 = mybir.dt.float8_e4m3fn_x4
ALU = mybir.AluOpType
ACT = mybir.ActivationFunctionType
AX = mybir.AxisListType

P = 128
S, CIN, COUT, V, T = 16, 512, 128, 32, 128
EPS = 1e-5
FLOPS = 2 * S * COUT * CIN * V * V + 2 * COUT * V * S * V * T
N_TILES = COUT // 4
RAW_BUFS = 6
TILES_T0, TILES_S1, TILES_T1, TILES_QG = 8, 6, 5, 2


def evenly(i, n, total):
    return (i + 1) * n // total > i * n // total


def tile_multiscale_gcn_pa_kernel(
    tc, ada_A, ada_w, ada_b, PA, feat, bn_gamma, bn_beta, bn_mean, bn_var, res, out
):
    nc = tc.nc
    with ExitStack() as ctx:
        const = ctx.enter_context(tc.tile_pool(name="const", bufs=1))
        keep = ctx.enter_context(tc.tile_pool(name="keep", bufs=1))
        big = ctx.enter_context(tc.tile_pool(name="big", bufs=1))
        raw_pool = ctx.enter_context(tc.tile_pool(name="rawp", bufs=RAW_BUFS))
        grp_pool = ctx.enter_context(tc.tile_pool(name="grpp", bufs=4))
        res_pool = ctx.enter_context(tc.tile_pool(name="resp", bufs=4))
        ps_m = ctx.enter_context(tc.psum_pool(name="psm", bufs=4))
        ps_t = ctx.enter_context(tc.psum_pool(name="pst", bufs=4))
        ctx.enter_context(tc.manual_schedule())

        w_codes = keep.tile([P, S * COUT], U32, align_bytes=64)
        w_scales = keep.tile([P, S * COUT], U8, align_bytes=64)
        a_codes = keep.tile([P, V * V], U32, align_bytes=64)
        a_scales = keep.tile([P, V * V], U8, align_bytes=64)
        g_codes = keep.tile([P, COUT * V], U32, align_bytes=64)
        g_scales = keep.tile([P, COUT * V], U8, align_bytes=64)
        f_codes = keep.tile([P, COUT * T], U32, align_bytes=64)
        f_scales = keep.tile([P, COUT * T], U8, align_bytes=64)

        zrows = const.tile([P, P], BF16)
        nc.vector.memset(zrows[:], 0.0)
        sq = const.tile([P, 2], F32)
        nc.vector.memset(sq[:], 1.0)
        nc.scalar.sqrt(out=sq[:, 1:2], in_=sq[:, 0:1])
        ident32 = const.tile([P, P], F32)
        make_identity(nc, ident32[:])
        identb = const.tile([P, P], BF16)
        make_identity(nc, identb[:])
        nc.scalar.dma_start(out=zrows[4:20, :], in_=ada_b)
        nc.scalar.dma_start(out=zrows[3:4, :], in_=bn_var.unsqueeze(0))
        nc.scalar.dma_start(out=zrows[0:1, :], in_=bn_gamma.unsqueeze(0))
        nc.scalar.dma_start(out=zrows[1:2, :], in_=bn_beta.unsqueeze(0))
        nc.scalar.dma_start(out=zrows[2:3, :], in_=bn_mean.unsqueeze(0))

        a2 = ada_A.rearrange("n i v w -> (n i) (v w)")
        raws = {}

        def load(kind, n):
            r = raw_pool.tile([P, 2048], BF16, tag="raw", name="raw")
            raws[(kind, n)] = r
            if kind == "a":
                r3 = r[:].rearrange("q (t c) -> q t c", t=4)
                for u in range(2):
                    nc.sync.dma_start(
                        out=r3[:, 2 * u : 2 * u + 2, :],
                        in_=a2[256 * u : 256 * u + 256, 512 * n : 512 * n + 512].rearrange(
                            "(q e) c -> q e c", e=2
                        ),
                    )
            elif kind == "w":
                nc.sync.dma_start(
                    out=r[:].rearrange("o (s i) -> o s i", s=4),
                    in_=ada_w[4 * n : 4 * n + 4].rearrange("s o i -> o s i"),
                )
            else:
                for c in range(4):
                    nc.sync.dma_start(
                        out=r[:, 512 * c : 512 * c + 512],
                        in_=feat[:, 0, 4 * n + c].rearrange("s (q j) t -> s q (j t)", j=4),
                    )

        loads = [("a", 0), ("w", 0), ("w", 1), ("w", 2), ("f", 0), ("w", 3), ("f", 1), ("a", 1)]
        loads.extend([("f", g) for g in range(2, N_TILES)])
        state = {"loaded": 0, "next": 0, "quantised": 0}

        def load_next():
            if state["loaded"] < len(loads):
                kind, n = loads[state["loaded"]]
                state["loaded"] += 1
                load(kind, n)

        for i in range(3):
            load_next()
        pa_full = const.tile([P, V * V], BF16)
        nc.sync.dma_start(
            out=pa_full[:],
            in_=PA.rearrange("s v w -> s (v w)").unsqueeze(1).to_broadcast([S, 8, V * V]),
        )
        for i in range(RAW_BUFS - 3):
            load_next()

        def regroup(dst, src, n, engine):
            if engine == "v":
                if n == 1:
                    nc.vector.tensor_copy(
                        out=dst.rearrange("p (c i t) -> p c t i", i=4, t=4),
                        in_=src.rearrange("p (t c i) -> p c t i", t=4, i=4),
                    )
                else:
                    nc.vector.tensor_copy(
                        out=dst.rearrange("p (n c i t) -> p n c t i", n=n, i=4, t=4),
                        in_=src.rearrange("p (n t c i) -> p n c t i", n=n, t=4, i=4),
                    )
            else:
                w = 2048 // n
                for b in range(n):
                    nc.scalar.copy(
                        out=dst[:, w * b : w * b + w].rearrange("p (c i t) -> p c t i", i=4, t=4),
                        in_=src[:, w * b : w * b + w].rearrange("p (t c i) -> p c t i", t=4, i=4),
                    )

        def quantise(codes, scales, c0, width, src):
            nc.vector.quantize_mx(
                out=codes[:, c0 : c0 + width].bitcast(FP8X4), scales=scales[:, c0 : c0 + width], in_=src
            )

        m8 = const.tile([P, 8], F32)
        nc.vector.tensor_reduce(
            out=m8[:], in_=ident32[:].rearrange("p (s w) -> p w s", w=8), axis=AX.X, op=ALU.add
        )
        m4 = const.tile([P, 4], F32)
        nc.vector.tensor_reduce(
            out=m4[:], in_=ident32[:].rearrange("p (o v) -> p o v", o=4), axis=AX.X, op=ALU.add
        )

        grp_a0 = grp_pool.tile([P, 2048], BF16, tag="grp", name="grp_a0", align_bytes=64)
        regroup(grp_a0[:], raws[("a", 0)][:], 1, "v")
        load_next()

        quantise(a_codes, a_scales, 0, 512, grp_a0[:])

        def w_transposes(c):
            r32 = raws[("w", c)][:].bitcast(F32)
            g = grp_pool.tile([P, 2048], BF16, tag="grp", name="grp_w", align_bytes=64)
            g32 = g[:].bitcast(F32)
            banks = []
            for a in range(2):
                wt = ps_t.tile([P, 512], F32, tag="tp", name="wt")
                banks.append(wt)
                for b in range(2):
                    for u in range(2):
                        col = (2 * a + b) * 256 + u * 128
                        nc.tensor.transpose(
                            wt[:, (2 * b + u) * 128 : (2 * b + u) * 128 + 128],
                            r32[:, col : col + 128],
                            ident32[:],
                        )
            for a in range(2):
                dst = g32[:, 512 * a : 512 * a + 512].rearrange("q (b o u) -> q b o u", b=2, u=2)
                src = banks[a][:].rearrange("q (b u o) -> q b o u", b=2, u=2)
                if a == 0:
                    nc.scalar.copy(out=dst, in_=src)
                else:
                    nc.vector.tensor_copy(out=dst, in_=src)
            load_next()
            return g

        grouped = {}

        def quantise_oldest():
            g = state["quantised"]
            state["quantised"] = g + 1
            quantise(f_codes, f_scales, 512 * g, 512, grouped[g][:])

        def feat_step(engine):
            g = state["next"]
            state["next"] = g + 1
            gt = grp_pool.tile([P, 2048], BF16, tag="grp", name="grp_f", align_bytes=64)
            regroup(gt[:], raws[("f", g)][:], 4, engine)
            load_next()
            grouped[g] = gt
            while state["quantised"] < g:
                quantise_oldest()

        def first_pass(h, s):
            acc = ps_m.tile([P, 512], F32, tag="mm", name="acc")
            nc.tensor.matmul_mx(
                out=acc[:],
                lhsT=w_codes[:, P * s : P * s + P].bitcast(FP8X4),
                lhsT_scale=w_scales[:, P * s : P * s + P],
                rhs=a_codes[:, 512 * h : 512 * h + 512].bitcast(FP8X4),
                rhs_scale=a_scales[:, 512 * h : 512 * h + 512],
                start=True,
                stop=True,
            )
            return acc

        def add_bias(xh, s, acc):
            nc.scalar.activation(
                out=xh[:].rearrange("o (v j s w) -> o v j s w", v=16, j=4, s=S)[:, :, :, s, :],
                in_=acc[:].rearrange("o (v w j) -> o v j w", v=16, j=4),
                func=ACT.Identity,
                bias=cst[:, 4 + s : 5 + s],
                scale=1.0,
            )

        in2 = big.tile([P, COUT * V * 4], BF16, tag="in2", name="in2", align_bytes=64)
        in2_v = in2[:].rearrange("p (g v o j) -> p g v o j", g=32, v=V, o=4)
        pa_t = const.tile([P, V * 4], F32)

        def transposes_and_pa(h, xh, n_tiles):
            for vl in range(16):
                v = 16 * h + vl
                tp = ps_t.tile([P, 512], F32, tag="tp", name="tp")
                for j in range(4):
                    col = (4 * vl + j) * P
                    nc.tensor.transpose(tp[:, P * j : P * j + P], xh[:, col : col + P], ident32[:])
                nc.vector.tensor_tensor(
                    out=in2_v[:, :, v, :, :],
                    in0=tp[:].rearrange("p (j g o) -> p g o j", j=4, o=4),
                    in1=pa_t[:, 4 * v : 4 * v + 4].unsqueeze(1).unsqueeze(1).to_broadcast([P, 32, 4, 4]),
                    op=ALU.mult,
                )
                if evenly(vl, n_tiles, 16):
                    feat_step("s")

        x0 = big.tile([P, 8192], F32, tag="x", name="x0")
        grp_w = w_transposes(0)
        quantise(w_codes, w_scales, 0, 512, grp_w[:])
        zt = ps_t.tile([P, P], BF16, tag="tp", name="zt")
        nc.tensor.transpose(zt[:], zrows[:], identb[:])
        cst = const.tile([P, 20], F32)
        nc.vector.tensor_copy(out=cst[:], in_=zt[:, 0:20])
        bn = const.tile([P, 8], F32)
        nc.vector.tensor_scalar_add(out=bn[:, 0:1], in0=cst[:, 3:4], scalar1=EPS)
        rep = const.tile([P, 2 * P], F32)
        scsh = const.tile([P, 64], F32)
        for c in range(4):
            if c < 3:
                grp_w = w_transposes(c + 1)
            if c == 2:
                rt = ps_t.tile([P, 2 * P], F32, tag="tp", name="rt")
                nc.tensor.transpose(rt[:, 0:P], rep[:, 0:P], ident32[:])
                nc.tensor.transpose(rt[:, P : 2 * P], rep[:, P : 2 * P], ident32[:])
            accs = [first_pass(0, s) for s in range(4 * c, 4 * c + 4)]
            if c == 1:
                nc.vector.reciprocal(out=bn[:, 1:2], in_=sq[:, 1:2])
                nc.vector.tensor_tensor(out=bn[:, 2:3], in0=cst[:, 0:1], in1=bn[:, 1:2], op=ALU.mult)
                nc.vector.tensor_tensor(out=bn[:, 3:4], in0=cst[:, 2:3], in1=bn[:, 2:3], op=ALU.mult)
                nc.vector.tensor_tensor(out=bn[:, 4:5], in0=cst[:, 1:2], in1=bn[:, 3:4], op=ALU.subtract)
                nc.vector.tensor_copy(out=rep[:, 0:P], in_=bn[:, 2:3].to_broadcast([P, P]))
                nc.vector.tensor_copy(out=rep[:, P : 2 * P], in_=bn[:, 4:5].to_broadcast([P, P]))
            if c == 3:
                bn_sel = const.tile([P, 2 * P], F32)
                nc.vector.tensor_tensor(
                    out=bn_sel[:].rearrange("p (c o) -> p c o", o=4),
                    in0=rt[:].rearrange("p (c o) -> p c o", o=4),
                    in1=m4[:].unsqueeze(1).to_broadcast([P, 64, 4]),
                    op=ALU.mult,
                )
                nc.vector.tensor_reduce(
                    out=scsh[:], in_=bn_sel[:].rearrange("p (c o) -> p c o", o=4), axis=AX.X, op=ALU.add
                )
            if c == 0:
                pa_sel = const.tile([P, V * V], F32)
                nc.vector.tensor_tensor(
                    out=pa_sel[:].rearrange("p (v j w) -> p v j w", v=V, j=4),
                    in0=pa_full[:].rearrange("p (v w j) -> p v j w", v=V, j=4),
                    in1=m8[:].unsqueeze(1).unsqueeze(1).to_broadcast([P, V, 4, 8]),
                    op=ALU.mult,
                )
                nc.vector.tensor_reduce(
                    out=pa_t[:], in_=pa_sel[:].rearrange("p (c w) -> p c w", w=8), axis=AX.X, op=ALU.add
                )
            if c < 3:
                quantise(w_codes, w_scales, 512 * (c + 1), 512, grp_w[:])
            for s in range(4 * c, 4 * c + 4):
                add_bias(x0, s, accs[s - 4 * c])
            if c == 0:
                nc.scalar.sqrt(out=sq[:, 1:2], in_=bn[:, 0:1])
            if c == 3:
                grp_a1 = grp_pool.tile([P, 2048], BF16, tag="grp", name="grp_a1", align_bytes=64)
                regroup(grp_a1[:], raws[("a", 1)][:], 1, "v")
                load_next()
            if c > 0:
                feat_step("v")
            if c == 3:
                feat_step("v")
        quantise(a_codes, a_scales, 512, 512, grp_a1[:])
        transposes_and_pa(0, x0, TILES_T0)
        x1 = big.tile([P, 8192], F32, tag="x", name="x1")
        for s in range(S):
            add_bias(x1, s, first_pass(1, s))
            if evenly(s, TILES_S1, S):
                feat_step("v")
        transposes_and_pa(1, x1, TILES_T1)
        for c in range(4):
            quantise(g_codes, g_scales, 1024 * c, 1024, in2[:, 4096 * c : 4096 * c + 4096])
            if evenly(c, TILES_QG, 4):
                feat_step("s")

        res_v = res.rearrange("n o v t -> (n o v) t").rearrange("(g p) t -> p g t", p=P)
        out_v = out.rearrange("n o v t -> (n o v) t").rearrange("(g p) t -> p g t", p=P)
        late = big.tile([P, 8192], F32, tag="x", name="late")
        res_tiles = {}

        def load_res(qd):
            if qd < 8:
                r = res_pool.tile([P, 4 * T], BF16, tag="res", name="res_t")
                nc.sync.dma_start(
                    out=r[:].rearrange("p (g t) -> p g t", g=4), in_=res_v[:, 4 * qd : 4 * qd + 4, :]
                )
                res_tiles[qd] = r

        def part(kind, qd):
            c0 = 2048 * kind + 512 * (qd % 3)
            return late[:, c0 : c0 + 512]

        def second_passes(qd):
            while state["quantised"] < 4 * qd + 4:
                quantise_oldest()
            banks = [ps_m.tile([P, 512], F32, tag="mm", name="s2") for o in range(4)]
            for k in range(4):
                g = 4 * qd + k
                for o in range(4):
                    ch = 4 * g + o
                    nc.tensor.matmul_mx(
                        out=banks[o][:, P * k : P * k + P],
                        lhsT=f_codes[:, P * ch : P * ch + P].bitcast(FP8X4),
                        lhsT_scale=f_scales[:, P * ch : P * ch + P],
                        rhs=g_codes[:, P * g : P * g + P].bitcast(FP8X4),
                        rhs_scale=g_scales[:, P * g : P * g + P],
                        start=True,
                        stop=True,
                    )
            for o in range(4):
                nc.scalar.copy(
                    out=part(0, qd).rearrange("t (k o v) -> t k o v", k=4, o=4)[:, :, o, :],
                    in_=banks[o][:].rearrange("t (k v o) -> t k v o", k=4, o=4)[:, :, :, o],
                )

        def back_and_norm(qd):
            ft = ps_t.tile([P, 512], F32, tag="tp", name="ft")
            for k in range(4):
                nc.tensor.transpose(
                    ft[:, P * k : P * k + P], part(0, qd)[:, P * k : P * k + P], ident32[:]
                )
            for k in range(4):
                g = 4 * qd + k
                nc.vector.scalar_tensor_tensor(
                    out=part(1, qd)[:, P * k : P * k + P],
                    in0=ft[:, P * k : P * k + P],
                    scalar=scsh[:, g : g + 1],
                    in1=res_tiles[qd][:, T * k : T * k + T],
                    op0=ALU.mult,
                    op1=ALU.add,
                )

        def relu_and_store(qd):
            for k in range(4):
                g = 4 * qd + k
                nc.scalar.activation(
                    out=part(2, qd)[:, P * k : P * k + P],
                    in_=part(1, qd)[:, P * k : P * k + P],
                    func=ACT.Relu,
                    bias=scsh[:, 32 + g : 33 + g],
                    scale=1.0,
                )
            nc.sync.dma_start(
                out=out_v[:, 4 * qd : 4 * qd + 4, :],
                in_=part(2, qd).rearrange("p (k t) -> p k t", k=4),
            )

        load_res(0)
        load_res(1)
        first_left = state["next"]
        left = N_TILES - first_left
        for i in range(10):
            if i < 8:
                want = max(4 * i + 4, first_left + ((i + 1) * left + 7) // 8)
                while state["next"] < want:
                    feat_step("s" if (state["next"] - first_left) % 3 == 2 else "v")
                load_res(i + 2)
                second_passes(i)
            if 1 <= i <= 8:
                back_and_norm(i - 1)
            if i >= 2:
                relu_and_store(i - 2)
